import numpy as np
import ml_dtypes

BF16 = ml_dtypes.bfloat16


def bf(x):
    return np.asarray(x, np.float32).astype(BF16)


def f32(x):
    return np.asarray(x, np.float32)


def f64(x):
    return np.asarray(x).astype(np.float64)


def striped(idx):
    return np.tile(idx.reshape(-1, 16).T, (8, 1))


C, S, K, T, L, N = 512, 512, 4, 16, 512, 2048


def setup_inputs():
    x = f32(np.random.uniform(size=(C, S)))
    w = f32(np.random.standard_normal((T, L)))
    w_comp = f32(np.random.standard_normal((T, L)))
    idx = np.concatenate([np.random.permutation(S) for _ in range(K)])
    return {"x": x, "w": w, "w_comp": w_comp, "offs": striped(idx)}


def reference(x, w, w_comp, offs):
    idx = offs[:16].T.reshape(-1)
    a = f64(x)[:, idx].reshape(C, K, L)
    sig = 1.0 / (1.0 + np.exp(f64(w_comp) - f64(w)))
    res = np.zeros((C, L))
    for t in range(T):
        p = np.ones((C, L))
        for i in range(K):
            bit = (t >> (K - 1 - i)) & 1
            p = p * (a[:, i, :] if bit else 1.0 - a[:, i, :])
        res = res + p * sig[t][None, :]
    return res

@@ -1,0 +1,76 @@
+import concourse.mybir as mybir
+from concourse.masks import make_identity
+
+F32 = mybir.dt.float32
+U16 = mybir.dt.uint16
+MULT = mybir.AluOpType.mult
+ADD = mybir.AluOpType.add
+SUBTRACT = mybir.AluOpType.subtract
+SIGMOID = mybir.ActivationFunctionType.Sigmoid
+
+P = 128
+SAMPLES = 512
+INPUTS = 512
+FAN_IN = 4
+ENTRIES = 16
+LUTS = 512
+LIST_COLS = LUTS // 16
+
+
+def tile_lutlayer_kernel(tc, x, w, w_comp, offs, out):
+    nc = tc.nc
+    with (
+        tc.tile_pool(name="held", bufs=1) as held,
+        tc.tile_pool(name="work", bufs=2) as work,
+        tc.psum_pool(name="psum", bufs=4) as psum,
+    ):
+        offsets = held.tile([P, FAN_IN * LIST_COLS], U16, name="offsets")
+        nc.sync.dma_start(offsets[:], offs)
+        w_rows = held.tile([ENTRIES, LUTS], F32, name="w_rows")
+        nc.scalar.dma_start(w_rows[:], w)
+        w_comp_rows = held.tile([ENTRIES, LUTS], F32, name="w_comp_rows")
+        nc.gpsimd.dma_start(w_comp_rows[:], w_comp)
+        x_blocks = []
+        for b in range(SAMPLES // P):
+            x_block = held.tile([P, INPUTS], F32, name=f"x_block{b}")
+            nc.sync.dma_start(x_block[:], x[b * P : (b + 1) * P, :])
+            x_blocks.append(x_block)
+
+        identity = held.tile([P, P], F32, name="identity")
+        make_identity(nc, identity[:])
+        to_coef = held.tile([P, ENTRIES], F32, name="to_coef")
+        nc.vector.tensor_copy(to_coef[:], identity[:, 0:ENTRIES])
+        for bit in range(FAN_IN):
+            pairs = to_coef[:].rearrange("t (g two h) -> t g two h", two=2, h=1 << bit)
+            nc.vector.tensor_tensor(pairs[:, :, 1:2, :], pairs[:, :, 1:2, :], pairs[:, :, 0:1, :], SUBTRACT)
+        to_coef_all = held.tile([P, ENTRIES, P], F32, name="to_coef_all")
+        nc.vector.tensor_copy(to_coef_all[:], to_coef[:].unsqueeze(2).to_broadcast([P, ENTRIES, P]))
+
+        sig = held.tile([P, LUTS], F32, name="sig")
+        nc.gpsimd.memset(sig[:], 0.0)
+        logit = held.tile([ENTRIES, LUTS], F32, name="logit")
+        nc.vector.tensor_tensor(logit[:], w_rows[:], w_comp_rows[:], SUBTRACT)
+        nc.scalar.activation(sig[0:ENTRIES, :], logit[:], SIGMOID)
+
+        coef = held.tile([P, ENTRIES, LUTS], F32, name="coef")
+        for s in list(range(ENTRIES // 2, ENTRIES)) + list(range(ENTRIES // 2)):
+            spread = psum.tile([P, LUTS], F32, name="spread")
+            nc.tensor.matmul(spread[:], to_coef_all[:, s, :], sig[:], start=True, stop=True)
+            nc.scalar.copy(coef[:, s, :], spread[:])
+
+        for b in range(SAMPLES // P):
+            cur = coef
+            for i in range(FAN_IN):
+                half = ENTRIES >> (i + 1)
+                product = work.tile([P, half, LUTS], F32, name=f"product{i}")
+                for k in range(half):
+                    nc.vector.tensor_tensor(
+                        product[:, k, :],
+                        x_blocks[b][:].indirect(offsets[:, i * LIST_COLS : (i + 1) * LIST_COLS]),
+                        cur[:, half + k, :],
+                        MULT,
+                    )
+                level = work.tile([P, half, LUTS], F32, name=f"level{i}")
+                nc.vector.tensor_tensor(level[:], cur[:, 0:half, :], product[:], ADD)
+                cur = level
+            nc.sync.dma_start(out[b * P : (b + 1) * P, :], cur[:, 0, :])

@@ -14,6 +14,7 @@ INPUTS = 512
 FAN_IN = 4
 ENTRIES = 16
 LUTS = 512
+IN_PSUM = 4
 LIST_COLS = LUTS // 16
 
 
@@ -22,7 +23,7 @@ def tile_lutlayer_kernel(tc, x, w, w_comp, offs, out):
     with (
         tc.tile_pool(name="held", bufs=1) as held,
         tc.tile_pool(name="work", bufs=2) as work,
-        tc.psum_pool(name="psum", bufs=4) as psum,
+        tc.psum_pool(name="psum", bufs=8) as psum,
     ):
         offsets = held.tile([P, FAN_IN * LIST_COLS], U16, name="offsets")
         nc.sync.dma_start(offsets[:], offs)
@@ -54,12 +55,15 @@ def tile_lutlayer_kernel(tc, x, w, w_comp, offs, out):
 
         coef = held.tile([P, ENTRIES, LUTS], F32, name="coef")
         for s in list(range(ENTRIES // 2, ENTRIES)) + list(range(ENTRIES // 2)):
-            spread = psum.tile([P, LUTS], F32, name="spread")
+            spread = psum.tile([P, LUTS], F32, name="spread", tag="bank")
             nc.tensor.matmul(spread[:], to_coef_all[:, s, :], sig[:], start=True, stop=True)
             nc.scalar.copy(coef[:, s, :], spread[:])
 
         for b in range(SAMPLES // P):
-            cur = coef
+            sums = [psum.tile([P, LUTS], F32, name=f"sum{k}", tag="bank") for k in range(IN_PSUM)]
+            for k in range(IN_PSUM):
+                nc.tensor.matmul(sums[k][:], identity[:], coef[:, k, :], start=True, stop=False)
+            multiplicands = coef[:, ENTRIES // 2 : ENTRIES, :]
             for i in range(FAN_IN):
                 half = ENTRIES >> (i + 1)
                 product = work.tile([P, half, LUTS], F32, name=f"product{i}")
@@ -67,10 +71,20 @@ def tile_lutlayer_kernel(tc, x, w, w_comp, offs, out):
                     nc.vector.tensor_tensor(
                         product[:, k, :],
                         x_blocks[b][:].indirect(offsets[:, i * LIST_COLS : (i + 1) * LIST_COLS]),
-                        cur[:, half + k, :],
+                        multiplicands[:, k, :],
                         MULT,
                     )
-                level = work.tile([P, half, LUTS], F32, name=f"level{i}")
-                nc.vector.tensor_tensor(level[:], cur[:, 0:half, :], product[:], ADD)
-                cur = level
-            nc.sync.dma_start(out[b * P : (b + 1) * P, :], cur[:, 0, :])
+                first_done = half // 2
+                done = work.tile([P, half - first_done, LUTS], F32, name=f"done{i}")
+                if half > IN_PSUM:
+                    nc.vector.tensor_tensor(
+                        done[:], coef[:, first_done:half, :], product[:, first_done:half, :], ADD
+                    )
+                for k in range(min(half, IN_PSUM)):
+                    nc.tensor.matmul(
+                        sums[k][:], identity[:], product[:, k, :], start=False, stop=(k >= first_done)
+                    )
+                    if k >= first_done:
+                        nc.scalar.copy(done[:, k - first_done, :], sums[k][:])
+                multiplicands = done[:]
+            nc.sync.dma_start(out[b * P : (b + 1) * P, :], multiplicands[:, 0, :])

@@ -14,7 +14,6 @@ INPUTS = 512
 FAN_IN = 4
 ENTRIES = 16
 LUTS = 512
-IN_PSUM = 4
 LIST_COLS = LUTS // 16
 
 
@@ -23,7 +22,7 @@ def tile_lutlayer_kernel(tc, x, w, w_comp, offs, out):
     with (
         tc.tile_pool(name="held", bufs=1) as held,
         tc.tile_pool(name="work", bufs=2) as work,
-        tc.psum_pool(name="psum", bufs=8) as psum,
+        tc.psum_pool(name="psum", bufs=4) as psum,
     ):
         offsets = held.tile([P, FAN_IN * LIST_COLS], U16, name="offsets")
         nc.sync.dma_start(offsets[:], offs)
@@ -55,15 +54,12 @@ def tile_lutlayer_kernel(tc, x, w, w_comp, offs, out):
 
         coef = held.tile([P, ENTRIES, LUTS], F32, name="coef")
         for s in list(range(ENTRIES // 2, ENTRIES)) + list(range(ENTRIES // 2)):
-            spread = psum.tile([P, LUTS], F32, name="spread", tag="bank")
+            spread = psum.tile([P, LUTS], F32, name="spread")
             nc.tensor.matmul(spread[:], to_coef_all[:, s, :], sig[:], start=True, stop=True)
             nc.scalar.copy(coef[:, s, :], spread[:])
 
         for b in range(SAMPLES // P):
-            sums = [psum.tile([P, LUTS], F32, name=f"sum{k}", tag="bank") for k in range(IN_PSUM)]
-            for k in range(IN_PSUM):
-                nc.tensor.matmul(sums[k][:], identity[:], coef[:, k, :], start=True, stop=False)
-            multiplicands = coef[:, ENTRIES // 2 : ENTRIES, :]
+            cur = coef
             for i in range(FAN_IN):
                 half = ENTRIES >> (i + 1)
                 product = work.tile([P, half, LUTS], F32, name=f"product{i}")
@@ -71,20 +67,10 @@ def tile_lutlayer_kernel(tc, x, w, w_comp, offs, out):
                     nc.vector.tensor_tensor(
                         product[:, k, :],
                         x_blocks[b][:].indirect(offsets[:, i * LIST_COLS : (i + 1) * LIST_COLS]),
-                        multiplicands[:, k, :],
+                        cur[:, half + k, :],
                         MULT,
                     )
-                first_done = half // 2
-                done = work.tile([P, half - first_done, LUTS], F32, name=f"done{i}")
-                if half > IN_PSUM:
-                    nc.vector.tensor_tensor(
-                        done[:], coef[:, first_done:half, :], product[:, first_done:half, :], ADD
-                    )
-                for k in range(min(half, IN_PSUM)):
-                    nc.tensor.matmul(
-                        sums[k][:], identity[:], product[:, k, :], start=False, stop=(k >= first_done)
-                    )
-                    if k >= first_done:
-                        nc.scalar.copy(done[:, k - first_done, :], sums[k][:])
-                multiplicands = done[:]
-            nc.sync.dma_start(out[b * P : (b + 1) * P, :], multiplicands[:, 0, :])
+                level = work.tile([P, half, LUTS], F32, name=f"level{i}")
+                nc.gpsimd.tensor_tensor(level[:], cur[:, 0:half, :], product[:], ADD)
+                cur = level
+            nc.sync.dma_start(out[b * P : (b + 1) * P, :], cur[:, 0, :])

@@ -6,6 +6,7 @@ U16 = mybir.dt.uint16
 MULT = mybir.AluOpType.mult
 ADD = mybir.AluOpType.add
 SUBTRACT = mybir.AluOpType.subtract
+NOT_EQUAL = mybir.AluOpType.not_equal
 SIGMOID = mybir.ActivationFunctionType.Sigmoid
 
 P = 128
@@ -15,62 +16,94 @@ FAN_IN = 4
 ENTRIES = 16
 LUTS = 512
 LIST_COLS = LUTS // 16
+GROUP = 4
+IN_PSUM = 2
 
 
 def tile_lutlayer_kernel(tc, x, w, w_comp, offs, out):
     nc = tc.nc
     with (
         tc.tile_pool(name="held", bufs=1) as held,
-        tc.tile_pool(name="work", bufs=2) as work,
-        tc.psum_pool(name="psum", bufs=4) as psum,
+        tc.tile_pool(name="work", bufs=4) as work,
+        tc.psum_pool(name="psum", bufs=8) as psum,
     ):
-        offsets = held.tile([P, FAN_IN * LIST_COLS], U16, name="offsets")
-        nc.sync.dma_start(offsets[:], offs)
         w_rows = held.tile([ENTRIES, LUTS], F32, name="w_rows")
         nc.scalar.dma_start(w_rows[:], w)
         w_comp_rows = held.tile([ENTRIES, LUTS], F32, name="w_comp_rows")
-        nc.gpsimd.dma_start(w_comp_rows[:], w_comp)
+        nc.sync.dma_start(w_comp_rows[:], w_comp)
+        offsets = held.tile([P, FAN_IN * LIST_COLS], U16, name="offsets")
+        nc.sync.dma_start(offsets[:], offs)
         x_blocks = []
         for b in range(SAMPLES // P):
             x_block = held.tile([P, INPUTS], F32, name=f"x_block{b}")
             nc.sync.dma_start(x_block[:], x[b * P : (b + 1) * P, :])
             x_blocks.append(x_block)
 
-        identity = held.tile([P, P], F32, name="identity")
-        make_identity(nc, identity[:])
         to_coef = held.tile([P, ENTRIES], F32, name="to_coef")
-        nc.vector.tensor_copy(to_coef[:], identity[:, 0:ENTRIES])
+        nc.gpsimd.memset(to_coef[:], 0.0)
+        nc.gpsimd.affine_select(
+            out=to_coef[:],
+            in_=to_coef[:],
+            compare_op=NOT_EQUAL,
+            fill=1.0,
+            base=0,
+            pattern=[[-1, ENTRIES]],
+            channel_multiplier=1,
+        )
         for bit in range(FAN_IN):
             pairs = to_coef[:].rearrange("t (g two h) -> t g two h", two=2, h=1 << bit)
             nc.vector.tensor_tensor(pairs[:, :, 1:2, :], pairs[:, :, 1:2, :], pairs[:, :, 0:1, :], SUBTRACT)
         to_coef_all = held.tile([P, ENTRIES, P], F32, name="to_coef_all")
-        nc.vector.tensor_copy(to_coef_all[:], to_coef[:].unsqueeze(2).to_broadcast([P, ENTRIES, P]))
+        for s_from in (ENTRIES // 2, 0):
+            s_to = s_from + ENTRIES // 2
+            nc.vector.tensor_copy(
+                to_coef_all[:, s_from:s_to, :],
+                to_coef[:, s_from:s_to].unsqueeze(2).to_broadcast([P, ENTRIES // 2, P]),
+            )
+        identity = held.tile([P, P], F32, name="identity")
+        make_identity(nc, identity[:])
 
         sig = held.tile([P, LUTS], F32, name="sig")
-        nc.gpsimd.memset(sig[:], 0.0)
+        nc.vector.memset(sig[:], 0.0)
         logit = held.tile([ENTRIES, LUTS], F32, name="logit")
         nc.vector.tensor_tensor(logit[:], w_rows[:], w_comp_rows[:], SUBTRACT)
         nc.scalar.activation(sig[0:ENTRIES, :], logit[:], SIGMOID)
 
         coef = held.tile([P, ENTRIES, LUTS], F32, name="coef")
-        for s in list(range(ENTRIES // 2, ENTRIES)) + list(range(ENTRIES // 2)):
-            spread = psum.tile([P, LUTS], F32, name="spread")
+        for s in list(range(ENTRIES // 2, ENTRIES)) + list(range(IN_PSUM, ENTRIES // 2)):
+            spread = psum.tile([P, LUTS], F32, name="spread", tag="bank")
             nc.tensor.matmul(spread[:], to_coef_all[:, s, :], sig[:], start=True, stop=True)
             nc.scalar.copy(coef[:, s, :], spread[:])
 
-        for b in range(SAMPLES // P):
-            cur = coef
+        for first_block in range(0, SAMPLES // P, GROUP):
+            blocks = range(first_block, first_block + GROUP)
+            sums = {}
+            value = {}
+            for b in blocks:
+                for k in range(IN_PSUM):
+                    sums[b, k] = psum.tile([P, LUTS], F32, name=f"sum{k}", tag="bank")
+                    nc.tensor.matmul(sums[b, k][:], to_coef_all[:, k, :], sig[:], start=True, stop=False)
+                value[b] = coef[:]
             for i in range(FAN_IN):
                 half = ENTRIES >> (i + 1)
-                product = work.tile([P, half, LUTS], F32, name=f"product{i}")
-                for k in range(half):
-                    nc.vector.tensor_tensor(
-                        product[:, k, :],
-                        x_blocks[b][:].indirect(offsets[:, i * LIST_COLS : (i + 1) * LIST_COLS]),
-                        cur[:, half + k, :],
-                        MULT,
-                    )
-                level = work.tile([P, half, LUTS], F32, name=f"level{i}")
-                nc.gpsimd.tensor_tensor(level[:], cur[:, 0:half, :], product[:], ADD)
-                cur = level
-            nc.sync.dma_start(out[b * P : (b + 1) * P, :], cur[:, 0, :])
+                for b in blocks:
+                    level = work.tile([P, half, LUTS], F32, name=f"level{i}")
+                    for k in range(half):
+                        nc.vector.tensor_tensor(
+                            level[:, k, :],
+                            x_blocks[b][:].indirect(offsets[:, i * LIST_COLS : (i + 1) * LIST_COLS]),
+                            value[b][:, half + k, :],
+                            MULT,
+                        )
+                    if half > IN_PSUM:
+                        nc.vector.tensor_tensor(
+                            level[:, IN_PSUM:half, :], value[b][:, IN_PSUM:half, :], level[:, IN_PSUM:half, :], ADD
+                        )
+                    for k in range(min(half, IN_PSUM)):
+                        complete = k >= half // 2
+                        nc.tensor.matmul(sums[b, k][:], identity[:], level[:, k, :], start=False, stop=complete)
+                        if complete:
+                            nc.scalar.copy(level[:, k, :], sums[b, k][:])
+                    value[b] = level[:]
+            for b in blocks:
+                nc.sync.dma_start(out[b * P : (b + 1) * P, :], value[b][:, 0, :])

@@ -16,8 +16,6 @@ FAN_IN = 4
 ENTRIES = 16
 LUTS = 512
 LIST_COLS = LUTS // 16
-GROUP = 4
-IN_PSUM = 2
 
 
 def tile_lutlayer_kernel(tc, x, w, w_comp, offs, out):
@@ -70,40 +68,49 @@ def tile_lutlayer_kernel(tc, x, w, w_comp, offs, out):
         nc.scalar.activation(sig[0:ENTRIES, :], logit[:], SIGMOID)
 
         coef = held.tile([P, ENTRIES, LUTS], F32, name="coef")
-        for s in list(range(ENTRIES // 2, ENTRIES)) + list(range(IN_PSUM, ENTRIES // 2)):
+        for s in reversed(range(ENTRIES // 4, ENTRIES)):
             spread = psum.tile([P, LUTS], F32, name="spread", tag="bank")
             nc.tensor.matmul(spread[:], to_coef_all[:, s, :], sig[:], start=True, stop=True)
             nc.scalar.copy(coef[:, s, :], spread[:])
 
-        for first_block in range(0, SAMPLES // P, GROUP):
-            blocks = range(first_block, first_block + GROUP)
-            sums = {}
-            value = {}
-            for b in blocks:
-                for k in range(IN_PSUM):
+        blocks = range(SAMPLES // P)
+        value = {b: coef[:] for b in blocks}
+        sums = {}
+
+        def one_level(b, i):
+            half = ENTRIES >> (i + 1)
+            first_of_pair = i % 2 == 0
+            quarter = half // 2 if first_of_pair else half
+            old = value[b]
+            level = work.tile([P, half, LUTS], F32, name=f"level{i}")
+            for k in reversed(range(half)):
+                nc.vector.tensor_tensor(
+                    level[:, k, :],
+                    x_blocks[b][:].indirect(offsets[:, i * LIST_COLS : (i + 1) * LIST_COLS]),
+                    old[:, half + k, :],
+                    MULT,
+                )
+            if first_of_pair:
+                nc.vector.tensor_tensor(
+                    level[:, quarter:half, :], old[:, quarter:half, :], level[:, quarter:half, :], ADD
+                )
+            for k in reversed(range(quarter)):
+                if first_of_pair:
                     sums[b, k] = psum.tile([P, LUTS], F32, name=f"sum{k}", tag="bank")
-                    nc.tensor.matmul(sums[b, k][:], to_coef_all[:, k, :], sig[:], start=True, stop=False)
-                value[b] = coef[:]
-            for i in range(FAN_IN):
-                half = ENTRIES >> (i + 1)
-                for b in blocks:
-                    level = work.tile([P, half, LUTS], F32, name=f"level{i}")
-                    for k in range(half):
-                        nc.vector.tensor_tensor(
-                            level[:, k, :],
-                            x_blocks[b][:].indirect(offsets[:, i * LIST_COLS : (i + 1) * LIST_COLS]),
-                            value[b][:, half + k, :],
-                            MULT,
-                        )
-                    if half > IN_PSUM:
-                        nc.vector.tensor_tensor(
-                            level[:, IN_PSUM:half, :], value[b][:, IN_PSUM:half, :], level[:, IN_PSUM:half, :], ADD
-                        )
-                    for k in range(min(half, IN_PSUM)):
-                        complete = k >= half // 2
-                        nc.tensor.matmul(sums[b, k][:], identity[:], level[:, k, :], start=False, stop=complete)
-                        if complete:
-                            nc.scalar.copy(level[:, k, :], sums[b, k][:])
-                    value[b] = level[:]
-            for b in blocks:
-                nc.sync.dma_start(out[b * P : (b + 1) * P, :], value[b][:, 0, :])
+                    if i == 0:
+                        nc.tensor.matmul(sums[b, k][:], to_coef_all[:, k, :], sig[:], start=True, stop=False)
+                    else:
+                        nc.tensor.matmul(sums[b, k][:], identity[:], old[:, k, :], start=True, stop=False)
+                nc.tensor.matmul(
+                    sums[b, k][:], identity[:], level[:, k, :], start=False, stop=not first_of_pair
+                )
+                if not first_of_pair:
+                    nc.scalar.copy(level[:, k, :], sums[b, k][:])
+            value[b] = level[:]
+
+        for side_by_side, levels in ((blocks[0:2], (0, 1)), (blocks[2:4], (0, 1)), (blocks, (2, 3))):
+            for i in levels:
+                for b in side_by_side:
+                    one_level(b, i)
+        for b in blocks:
+            nc.sync.dma_start(out[b * P : (b + 1) * P, :], value[b][:, 0, :])

@@ -16,6 +16,7 @@ FAN_IN = 4
 ENTRIES = 16
 LUTS = 512
 LIST_COLS = LUTS // 16
+IN_PSUM = 4
 
 
 def tile_lutlayer_kernel(tc, x, w, w_comp, offs, out):
@@ -68,7 +69,7 @@ def tile_lutlayer_kernel(tc, x, w, w_comp, offs, out):
         nc.scalar.activation(sig[0:ENTRIES, :], logit[:], SIGMOID)
 
         coef = held.tile([P, ENTRIES, LUTS], F32, name="coef")
-        for s in reversed(range(ENTRIES // 4, ENTRIES)):
+        for s in reversed(range(IN_PSUM, ENTRIES)):
             spread = psum.tile([P, LUTS], F32, name="spread", tag="bank")
             nc.tensor.matmul(spread[:], to_coef_all[:, s, :], sig[:], start=True, stop=True)
             nc.scalar.copy(coef[:, s, :], spread[:])
@@ -79,38 +80,35 @@ def tile_lutlayer_kernel(tc, x, w, w_comp, offs, out):
 
         def one_level(b, i):
             half = ENTRIES >> (i + 1)
-            first_of_pair = i % 2 == 0
-            quarter = half // 2 if first_of_pair else half
-            old = value[b]
+            in_psum = IN_PSUM if i < 2 else 0
             level = work.tile([P, half, LUTS], F32, name=f"level{i}")
             for k in reversed(range(half)):
                 nc.vector.tensor_tensor(
                     level[:, k, :],
                     x_blocks[b][:].indirect(offsets[:, i * LIST_COLS : (i + 1) * LIST_COLS]),
-                    old[:, half + k, :],
+                    value[b][:, half + k, :],
                     MULT,
                 )
-            if first_of_pair:
+            if half > in_psum:
                 nc.vector.tensor_tensor(
-                    level[:, quarter:half, :], old[:, quarter:half, :], level[:, quarter:half, :], ADD
+                    level[:, in_psum:half, :], value[b][:, in_psum:half, :], level[:, in_psum:half, :], ADD
                 )
-            for k in reversed(range(quarter)):
-                if first_of_pair:
-                    sums[b, k] = psum.tile([P, LUTS], F32, name=f"sum{k}", tag="bank")
-                    if i == 0:
-                        nc.tensor.matmul(sums[b, k][:], to_coef_all[:, k, :], sig[:], start=True, stop=False)
-                    else:
-                        nc.tensor.matmul(sums[b, k][:], identity[:], old[:, k, :], start=True, stop=False)
-                nc.tensor.matmul(
-                    sums[b, k][:], identity[:], level[:, k, :], start=False, stop=not first_of_pair
-                )
-                if not first_of_pair:
+            for k in reversed(range(in_psum)):
+                nc.tensor.matmul(sums[b, k][:], identity[:], level[:, k, :], start=False, stop=(i == 1))
+                if i == 1:
                     nc.scalar.copy(level[:, k, :], sums[b, k][:])
             value[b] = level[:]
 
-        for side_by_side, levels in ((blocks[0:2], (0, 1)), (blocks[2:4], (0, 1)), (blocks, (2, 3))):
-            for i in levels:
-                for b in side_by_side:
+        for pair in (blocks[0:2], blocks[2:4]):
+            for b in pair:
+                for k in range(IN_PSUM):
+                    sums[b, k] = psum.tile([P, LUTS], F32, name=f"sum{k}", tag="bank")
+                    nc.tensor.matmul(sums[b, k][:], to_coef_all[:, k, :], sig[:], start=True, stop=False)
+            for i in (0, 1):
+                for b in pair:
                     one_level(b, i)
+        for i in (2, 3):
+            for b in blocks:
+                one_level(b, i)
         for b in blocks:
             nc.sync.dma_start(out[b * P : (b + 1) * P, :], value[b][:, 0, :])

@@ -16,7 +16,6 @@ FAN_IN = 4
 ENTRIES = 16
 LUTS = 512
 LIST_COLS = LUTS // 16
-IN_PSUM = 4
 
 
 def tile_lutlayer_kernel(tc, x, w, w_comp, offs, out):
@@ -69,7 +68,7 @@ def tile_lutlayer_kernel(tc, x, w, w_comp, offs, out):
         nc.scalar.activation(sig[0:ENTRIES, :], logit[:], SIGMOID)
 
         coef = held.tile([P, ENTRIES, LUTS], F32, name="coef")
-        for s in reversed(range(IN_PSUM, ENTRIES)):
+        for s in reversed(range(ENTRIES // 4, ENTRIES)):
             spread = psum.tile([P, LUTS], F32, name="spread", tag="bank")
             nc.tensor.matmul(spread[:], to_coef_all[:, s, :], sig[:], start=True, stop=True)
             nc.scalar.copy(coef[:, s, :], spread[:])
@@ -80,35 +79,42 @@ def tile_lutlayer_kernel(tc, x, w, w_comp, offs, out):
 
         def one_level(b, i):
             half = ENTRIES >> (i + 1)
-            in_psum = IN_PSUM if i < 2 else 0
+            first_of_pair = i % 2 == 0
+            if i == FAN_IN - 1:
+                by_tensor = 0
+            elif first_of_pair:
+                by_tensor = half // 2
+            else:
+                by_tensor = half
+            sum_is_complete = not first_of_pair or i == FAN_IN - 2
+            old = value[b]
             level = work.tile([P, half, LUTS], F32, name=f"level{i}")
             for k in reversed(range(half)):
                 nc.vector.tensor_tensor(
                     level[:, k, :],
                     x_blocks[b][:].indirect(offsets[:, i * LIST_COLS : (i + 1) * LIST_COLS]),
-                    value[b][:, half + k, :],
+                    old[:, half + k, :],
                     MULT,
                 )
-            if half > in_psum:
+            if by_tensor < half:
                 nc.vector.tensor_tensor(
-                    level[:, in_psum:half, :], value[b][:, in_psum:half, :], level[:, in_psum:half, :], ADD
+                    level[:, by_tensor:half, :], old[:, by_tensor:half, :], level[:, by_tensor:half, :], ADD
                 )
-            for k in reversed(range(in_psum)):
-                nc.tensor.matmul(sums[b, k][:], identity[:], level[:, k, :], start=False, stop=(i == 1))
-                if i == 1:
+            for k in reversed(range(by_tensor)):
+                if first_of_pair:
+                    sums[b, k] = psum.tile([P, LUTS], F32, name=f"sum{k}", tag="bank")
+                    if i == 0:
+                        nc.tensor.matmul(sums[b, k][:], to_coef_all[:, k, :], sig[:], start=True, stop=False)
+                    else:
+                        nc.tensor.matmul(sums[b, k][:], identity[:], old[:, k, :], start=True, stop=False)
+                nc.tensor.matmul(sums[b, k][:], identity[:], level[:, k, :], start=False, stop=sum_is_complete)
+                if sum_is_complete:
                     nc.scalar.copy(level[:, k, :], sums[b, k][:])
             value[b] = level[:]
 
-        for pair in (blocks[0:2], blocks[2:4]):
-            for b in pair:
-                for k in range(IN_PSUM):
-                    sums[b, k] = psum.tile([P, LUTS], F32, name=f"sum{k}", tag="bank")
-                    nc.tensor.matmul(sums[b, k][:], to_coef_all[:, k, :], sig[:], start=True, stop=False)
-            for i in (0, 1):
-                for b in pair:
+        for side_by_side, levels in ((blocks[0:2], (0, 1)), (blocks[2:4], (0, 1)), (blocks, (2, 3))):
+            for i in levels:
+                for b in side_by_side:
                     one_level(b, i)
-        for i in (2, 3):
-            for b in blocks:
-                one_level(b, i)
         for b in blocks:
             nc.sync.dma_start(out[b * P : (b + 1) * P, :], value[b][:, 0, :])

@@ -2,119 +2,180 @@ import concourse.mybir as mybir
 from concourse.masks import make_identity
 
 F32 = mybir.dt.float32
+BF16 = mybir.dt.bfloat16
 U16 = mybir.dt.uint16
 MULT = mybir.AluOpType.mult
 ADD = mybir.AluOpType.add
 SUBTRACT = mybir.AluOpType.subtract
 NOT_EQUAL = mybir.AluOpType.not_equal
+IS_GE = mybir.AluOpType.is_ge
 SIGMOID = mybir.ActivationFunctionType.Sigmoid
 
 P = 128
 SAMPLES = 512
+BLOCKS = SAMPLES // P
 INPUTS = 512
 FAN_IN = 4
 ENTRIES = 16
 LUTS = 512
 LIST_COLS = LUTS // 16
+LATE = ENTRIES // 4
+PARTS = 3
+ROWS = PARTS * ENTRIES
+BY_VECTOR = 1
 
 
 def tile_lutlayer_kernel(tc, x, w, w_comp, offs, out):
     nc = tc.nc
     with (
         tc.tile_pool(name="held", bufs=1) as held,
-        tc.tile_pool(name="work", bufs=4) as work,
+        tc.tile_pool(name="work", bufs=2) as work,
         tc.psum_pool(name="psum", bufs=8) as psum,
     ):
-        w_rows = held.tile([ENTRIES, LUTS], F32, name="w_rows")
-        nc.scalar.dma_start(w_rows[:], w)
-        w_comp_rows = held.tile([ENTRIES, LUTS], F32, name="w_comp_rows")
-        nc.sync.dma_start(w_comp_rows[:], w_comp)
+        w_rows = held.tile([ROWS, LUTS], F32, name="w_rows")
+        w_comp_rows = held.tile([ROWS, LUTS], F32, name="w_comp_rows")
+        for part in range(PARTS):
+            nc.scalar.dma_start(w_rows[part * ENTRIES : (part + 1) * ENTRIES, :], w)
+            nc.sync.dma_start(w_comp_rows[part * ENTRIES : (part + 1) * ENTRIES, :], w_comp)
         offsets = held.tile([P, FAN_IN * LIST_COLS], U16, name="offsets")
         nc.sync.dma_start(offsets[:], offs)
         x_blocks = []
-        for b in range(SAMPLES // P):
+        for b in range(BLOCKS):
             x_block = held.tile([P, INPUTS], F32, name=f"x_block{b}")
             nc.sync.dma_start(x_block[:], x[b * P : (b + 1) * P, :])
             x_blocks.append(x_block)
 
+        warm_up = held.tile([P, 2], F32, name="warm_up")
+        nc.gpsimd.memset(warm_up[:], 0.0)
+        nc.scalar.activation(warm_up[:, 1:2], warm_up[:, 0:1], SIGMOID)
+
         to_coef = held.tile([P, ENTRIES], F32, name="to_coef")
         nc.gpsimd.memset(to_coef[:], 0.0)
-        nc.gpsimd.affine_select(
-            out=to_coef[:],
-            in_=to_coef[:],
-            compare_op=NOT_EQUAL,
-            fill=1.0,
-            base=0,
-            pattern=[[-1, ENTRIES]],
-            channel_multiplier=1,
-        )
+        for part in range(PARTS):
+            nc.gpsimd.affine_select(
+                out=to_coef[:],
+                in_=to_coef[:],
+                compare_op=NOT_EQUAL,
+                fill=1.0,
+                base=-part * ENTRIES,
+                pattern=[[-1, ENTRIES]],
+                channel_multiplier=1,
+            )
         for bit in range(FAN_IN):
             pairs = to_coef[:].rearrange("t (g two h) -> t g two h", two=2, h=1 << bit)
             nc.vector.tensor_tensor(pairs[:, :, 1:2, :], pairs[:, :, 1:2, :], pairs[:, :, 0:1, :], SUBTRACT)
-        to_coef_all = held.tile([P, ENTRIES, P], F32, name="to_coef_all")
-        for s_from in (ENTRIES // 2, 0):
+        minus_from = held.tile([P, PARTS - 1], F32, name="minus_from")
+        nc.gpsimd.memset(minus_from[:], -1.0)
+        nc.gpsimd.affine_select(
+            out=minus_from[:],
+            in_=minus_from[:],
+            compare_op=IS_GE,
+            fill=0.0,
+            base=-ENTRIES,
+            pattern=[[-ENTRIES, PARTS - 1]],
+            channel_multiplier=1,
+        )
+        sig_parts = held.tile([P, LUTS], BF16, name="sig_parts")
+        nc.gpsimd.memset(sig_parts[:], 0.0)
+        to_coef_all = held.tile([P, ENTRIES, P], BF16, name="to_coef_all")
+        for engine, s_from in ((nc.vector, ENTRIES // 2), (nc.gpsimd, 0)):
             s_to = s_from + ENTRIES // 2
-            nc.vector.tensor_copy(
+            engine.tensor_copy(
                 to_coef_all[:, s_from:s_to, :],
                 to_coef[:, s_from:s_to].unsqueeze(2).to_broadcast([P, ENTRIES // 2, P]),
             )
         identity = held.tile([P, P], F32, name="identity")
         make_identity(nc, identity[:])
 
-        sig = held.tile([P, LUTS], F32, name="sig")
-        nc.vector.memset(sig[:], 0.0)
-        logit = held.tile([ENTRIES, LUTS], F32, name="logit")
+        logit = held.tile([ROWS, LUTS], F32, name="logit")
         nc.vector.tensor_tensor(logit[:], w_rows[:], w_comp_rows[:], SUBTRACT)
-        nc.scalar.activation(sig[0:ENTRIES, :], logit[:], SIGMOID)
+        sig = held.tile([ROWS, LUTS], F32, name="sig")
+        nc.scalar.activation(sig[:], logit[:], SIGMOID)
+        head = held.tile([ROWS, LUTS], BF16, name="head")
+        nc.vector.tensor_copy(head[:], sig[:])
+        after_head = held.tile([ROWS, LUTS], F32, name="after_head")
+        nc.vector.scalar_tensor_tensor(after_head[:], head[:], minus_from[0:ROWS, 0:1], sig[:], MULT, ADD)
+        middle = held.tile([ROWS, LUTS], BF16, name="middle")
+        nc.vector.tensor_copy(middle[:], after_head[:])
+        nc.vector.scalar_tensor_tensor(
+            sig_parts[0:ROWS, :], middle[:], minus_from[0:ROWS, 1:2], after_head[:], MULT, ADD
+        )
 
         coef = held.tile([P, ENTRIES, LUTS], F32, name="coef")
-        for s in reversed(range(ENTRIES // 4, ENTRIES)):
+        multiplied_at_level_0 = list(reversed(range(ENTRIES // 2, ENTRIES)))
+        for s in multiplied_at_level_0 + list(range(LATE, LATE + BY_VECTOR)):
             spread = psum.tile([P, LUTS], F32, name="spread", tag="bank")
-            nc.tensor.matmul(spread[:], to_coef_all[:, s, :], sig[:], start=True, stop=True)
+            nc.tensor.matmul(spread[:], to_coef_all[:, s, :], sig_parts[:], start=True, stop=True)
             nc.scalar.copy(coef[:, s, :], spread[:])
 
-        blocks = range(SAMPLES // P)
-        value = {b: coef[:] for b in blocks}
+        factors = {}
         sums = {}
+        all_but_last = {}
 
-        def one_level(b, i):
-            half = ENTRIES >> (i + 1)
-            first_of_pair = i % 2 == 0
-            if i == FAN_IN - 1:
-                by_tensor = 0
-            elif first_of_pair:
-                by_tensor = half // 2
-            else:
-                by_tensor = half
-            sum_is_complete = not first_of_pair or i == FAN_IN - 2
-            old = value[b]
-            level = work.tile([P, half, LUTS], F32, name=f"level{i}")
-            for k in reversed(range(half)):
+        def multiply(b, i, count):
+            products = work.tile([P, count, LUTS], F32, name=f"products{i}", bufs=1 if i == 0 else 2)
+            for k in reversed(range(count)):
                 nc.vector.tensor_tensor(
-                    level[:, k, :],
+                    products[:, k, :],
                     x_blocks[b][:].indirect(offsets[:, i * LIST_COLS : (i + 1) * LIST_COLS]),
-                    old[:, half + k, :],
+                    factors[b][:, k, :],
                     MULT,
                 )
-            if by_tensor < half:
-                nc.vector.tensor_tensor(
-                    level[:, by_tensor:half, :], old[:, by_tensor:half, :], level[:, by_tensor:half, :], ADD
-                )
-            for k in reversed(range(by_tensor)):
-                if first_of_pair:
-                    sums[b, k] = psum.tile([P, LUTS], F32, name=f"sum{k}", tag="bank")
-                    if i == 0:
-                        nc.tensor.matmul(sums[b, k][:], to_coef_all[:, k, :], sig[:], start=True, stop=False)
-                    else:
-                        nc.tensor.matmul(sums[b, k][:], identity[:], old[:, k, :], start=True, stop=False)
-                nc.tensor.matmul(sums[b, k][:], identity[:], level[:, k, :], start=False, stop=sum_is_complete)
-                if sum_is_complete:
-                    nc.scalar.copy(level[:, k, :], sums[b, k][:])
-            value[b] = level[:]
+            return products
 
-        for side_by_side, levels in ((blocks[0:2], (0, 1)), (blocks[2:4], (0, 1)), (blocks, (2, 3))):
-            for i in levels:
-                for b in side_by_side:
-                    one_level(b, i)
-        for b in blocks:
-            nc.sync.dma_start(out[b * P : (b + 1) * P, :], value[b][:, 0, :])
+        def open_sum(k):
+            bank = psum.tile([P, LUTS], F32, name="bank")
+            nc.tensor.matmul(bank[:], to_coef_all[:, k, :], sig_parts[:], start=True, stop=False)
+            return bank
+
+        def add_term(bank, term, last):
+            nc.tensor.matmul(bank[:], identity[:], term, start=False, stop=last)
+
+        def level_0(b):
+            factors[b] = coef[:, ENTRIES // 2 : ENTRIES, :]
+            products = multiply(b, 0, ENTRIES // 2)
+            finished = work.tile([P, LATE, LUTS], F32, name="finished0")
+            for k in reversed(range(LATE + BY_VECTOR, 2 * LATE)):
+                bank = open_sum(k)
+                add_term(bank, products[:, k, :], last=True)
+                nc.scalar.copy(finished[:, k - LATE, :], bank[:])
+            nc.vector.tensor_tensor(
+                finished[:, 0:BY_VECTOR, :],
+                coef[:, LATE : LATE + BY_VECTOR, :],
+                products[:, LATE : LATE + BY_VECTOR, :],
+                ADD,
+            )
+            for k in reversed(range(LATE)):
+                sums[b, k] = open_sum(k)
+                add_term(sums[b, k], products[:, k, :], last=False)
+            factors[b] = finished[:]
+
+        def level_1(b):
+            products = multiply(b, 1, 4)
+            finished = work.tile([P, 2, LUTS], F32, name="finished1")
+            for k in reversed(range(4)):
+                add_term(sums[b, k], products[:, k, :], last=k >= 2)
+                if k >= 2:
+                    nc.scalar.copy(finished[:, k - 2, :], sums[b, k][:])
+            factors[b] = finished[:]
+
+        def level_2(b):
+            products = multiply(b, 2, 2)
+            finished = work.tile([P, 2, LUTS], F32, name="finished2")
+            for k in reversed(range(2)):
+                add_term(sums[b, k], products[:, k, :], last=True)
+                nc.scalar.copy(finished[:, k, :], sums[b, k][:])
+            factors[b] = finished[:, 1:2, :]
+            all_but_last[b] = finished[:, 0, :]
+
+        def level_3(b):
+            products = multiply(b, 3, 1)
+            nc.vector.tensor_tensor(products[:, 0, :], all_but_last[b], products[:, 0, :], ADD)
+            nc.sync.dma_start(out[b * P : (b + 1) * P, :], products[:, 0, :])
+
+        take_level = {0: level_0, 1: level_1, 2: level_2, 3: level_3}
+        for step in range(BLOCKS + FAN_IN - 1):
+            for i in (1, 2, 0, 3):
+                b = step - i
+                if 0 <= b < BLOCKS:
+                    take_level[i](b)

@@ -22,7 +22,6 @@ LIST_COLS = LUTS // 16
 LATE = ENTRIES // 4
 PARTS = 3
 ROWS = PARTS * ENTRIES
-BY_VECTOR = 1
 
 
 def tile_lutlayer_kernel(tc, x, w, w_comp, offs, out):
@@ -102,8 +101,7 @@ def tile_lutlayer_kernel(tc, x, w, w_comp, offs, out):
         )
 
         coef = held.tile([P, ENTRIES, LUTS], F32, name="coef")
-        multiplied_at_level_0 = list(reversed(range(ENTRIES // 2, ENTRIES)))
-        for s in multiplied_at_level_0 + list(range(LATE, LATE + BY_VECTOR)):
+        for s in reversed(range(ENTRIES // 2, ENTRIES)):
             spread = psum.tile([P, LUTS], F32, name="spread", tag="bank")
             nc.tensor.matmul(spread[:], to_coef_all[:, s, :], sig_parts[:], start=True, stop=True)
             nc.scalar.copy(coef[:, s, :], spread[:])
@@ -135,16 +133,10 @@ def tile_lutlayer_kernel(tc, x, w, w_comp, offs, out):
             factors[b] = coef[:, ENTRIES // 2 : ENTRIES, :]
             products = multiply(b, 0, ENTRIES // 2)
             finished = work.tile([P, LATE, LUTS], F32, name="finished0")
-            for k in reversed(range(LATE + BY_VECTOR, 2 * LATE)):
+            for k in reversed(range(LATE, 2 * LATE)):
                 bank = open_sum(k)
                 add_term(bank, products[:, k, :], last=True)
                 nc.scalar.copy(finished[:, k - LATE, :], bank[:])
-            nc.vector.tensor_tensor(
-                finished[:, 0:BY_VECTOR, :],
-                coef[:, LATE : LATE + BY_VECTOR, :],
-                products[:, LATE : LATE + BY_VECTOR, :],
-                ADD,
-            )
             for k in reversed(range(LATE)):
                 sums[b, k] = open_sum(k)
                 add_term(sums[b, k], products[:, k, :], last=False)

@@ -62,7 +62,7 @@ def tile_lutlayer_kernel(tc, x, w, w_comp, offs, out):
             )
         for bit in range(FAN_IN):
             pairs = to_coef[:].rearrange("t (g two h) -> t g two h", two=2, h=1 << bit)
-            nc.vector.tensor_tensor(pairs[:, :, 1:2, :], pairs[:, :, 1:2, :], pairs[:, :, 0:1, :], SUBTRACT)
+            nc.gpsimd.tensor_tensor(pairs[:, :, 1:2, :], pairs[:, :, 1:2, :], pairs[:, :, 0:1, :], SUBTRACT)
         minus_from = held.tile([P, PARTS - 1], F32, name="minus_from")
         nc.gpsimd.memset(minus_from[:], -1.0)
         nc.gpsimd.affine_select(
@@ -77,12 +77,9 @@ def tile_lutlayer_kernel(tc, x, w, w_comp, offs, out):
         sig_parts = held.tile([P, LUTS], BF16, name="sig_parts")
         nc.gpsimd.memset(sig_parts[:], 0.0)
         to_coef_all = held.tile([P, ENTRIES, P], BF16, name="to_coef_all")
-        for engine, s_from in ((nc.vector, ENTRIES // 2), (nc.gpsimd, 0)):
-            s_to = s_from + ENTRIES // 2
-            engine.tensor_copy(
-                to_coef_all[:, s_from:s_to, :],
-                to_coef[:, s_from:s_to].unsqueeze(2).to_broadcast([P, ENTRIES // 2, P]),
-            )
+        half = ENTRIES // 2
+        nc.scalar.copy(to_coef_all[:, half:ENTRIES, :], to_coef[:, half:ENTRIES].unsqueeze(2).to_broadcast([P, half, P]))
+        nc.gpsimd.tensor_copy(to_coef_all[:, 0:half, :], to_coef[:, 0:half].unsqueeze(2).to_broadcast([P, half, P]))
         identity = held.tile([P, P], F32, name="identity")
         make_identity(nc, identity[:])
 
@@ -167,7 +164,7 @@ def tile_lutlayer_kernel(tc, x, w, w_comp, offs, out):
 
         take_level = {0: level_0, 1: level_1, 2: level_2, 3: level_3}
         for step in range(BLOCKS + FAN_IN - 1):
-            for i in (1, 2, 0, 3):
+            for i in (2, 3, 1, 0):
                 b = step - i
                 if 0 <= b < BLOCKS:
                     take_level[i](b)

@@ -44,10 +44,6 @@ def tile_lutlayer_kernel(tc, x, w, w_comp, offs, out):
             nc.sync.dma_start(x_block[:], x[b * P : (b + 1) * P, :])
             x_blocks.append(x_block)
 
-        warm_up = held.tile([P, 2], F32, name="warm_up")
-        nc.gpsimd.memset(warm_up[:], 0.0)
-        nc.scalar.activation(warm_up[:, 1:2], warm_up[:, 0:1], SIGMOID)
-
         to_coef = held.tile([P, ENTRIES], F32, name="to_coef")
         nc.gpsimd.memset(to_coef[:], 0.0)
         for part in range(PARTS):

@@ -17,11 +17,12 @@ BLOCKS = SAMPLES // P
 INPUTS = 512
 FAN_IN = 4
 ENTRIES = 16
+UPPER = ENTRIES // 2
 LUTS = 512
 LIST_COLS = LUTS // 16
-LATE = ENTRIES // 4
 PARTS = 3
 ROWS = PARTS * ENTRIES
+BANKS = 8
 
 
 def tile_lutlayer_kernel(tc, x, w, w_comp, offs, out):
@@ -29,7 +30,7 @@ def tile_lutlayer_kernel(tc, x, w, w_comp, offs, out):
     with (
         tc.tile_pool(name="held", bufs=1) as held,
         tc.tile_pool(name="work", bufs=2) as work,
-        tc.psum_pool(name="psum", bufs=8) as psum,
+        tc.psum_pool(name="psum", bufs=BANKS) as psum,
     ):
         w_rows = held.tile([ROWS, LUTS], F32, name="w_rows")
         w_comp_rows = held.tile([ROWS, LUTS], F32, name="w_comp_rows")
@@ -72,17 +73,19 @@ def tile_lutlayer_kernel(tc, x, w, w_comp, offs, out):
         )
         sig_parts = held.tile([P, LUTS], BF16, name="sig_parts")
         nc.gpsimd.memset(sig_parts[:], 0.0)
-        to_coef_all = held.tile([P, ENTRIES, P], BF16, name="to_coef_all")
-        half = ENTRIES // 2
-        nc.scalar.copy(to_coef_all[:, half:ENTRIES, :], to_coef[:, half:ENTRIES].unsqueeze(2).to_broadcast([P, half, P]))
-        nc.gpsimd.tensor_copy(to_coef_all[:, 0:half, :], to_coef[:, 0:half].unsqueeze(2).to_broadcast([P, half, P]))
         identity = held.tile([P, P], F32, name="identity")
         make_identity(nc, identity[:])
+
+        to_coef_all = held.tile([P, ENTRIES, P], BF16, name="to_coef_all")
+        nc.scalar.copy(
+            to_coef_all[:, UPPER:ENTRIES, :], to_coef[:, UPPER:ENTRIES].unsqueeze(2).to_broadcast([P, UPPER, P])
+        )
 
         logit = held.tile([ROWS, LUTS], F32, name="logit")
         nc.vector.tensor_tensor(logit[:], w_rows[:], w_comp_rows[:], SUBTRACT)
         sig = held.tile([ROWS, LUTS], F32, name="sig")
         nc.scalar.activation(sig[:], logit[:], SIGMOID)
+        nc.scalar.copy(to_coef_all[:, 0:UPPER, :], to_coef[:, 0:UPPER].unsqueeze(2).to_broadcast([P, UPPER, P]))
         head = held.tile([ROWS, LUTS], BF16, name="head")
         nc.vector.tensor_copy(head[:], sig[:])
         after_head = held.tile([ROWS, LUTS], F32, name="after_head")
@@ -93,26 +96,6 @@ def tile_lutlayer_kernel(tc, x, w, w_comp, offs, out):
             sig_parts[0:ROWS, :], middle[:], minus_from[0:ROWS, 1:2], after_head[:], MULT, ADD
         )
 
-        coef = held.tile([P, ENTRIES, LUTS], F32, name="coef")
-        for s in reversed(range(ENTRIES // 2, ENTRIES)):
-            spread = psum.tile([P, LUTS], F32, name="spread", tag="bank")
-            nc.tensor.matmul(spread[:], to_coef_all[:, s, :], sig_parts[:], start=True, stop=True)
-            nc.scalar.copy(coef[:, s, :], spread[:])
-
-        factors = {}
-        sums = {}
-        all_but_last = {}
-
-        def multiply(b, i, count):
-            products = work.tile([P, count, LUTS], F32, name=f"products{i}", bufs=1 if i == 0 else 2)
-            for k in reversed(range(count)):
-                nc.vector.tensor_tensor(
-                    products[:, k, :],
-                    x_blocks[b][:].indirect(offsets[:, i * LIST_COLS : (i + 1) * LIST_COLS]),
-                    factors[b][:, k, :],
-                    MULT,
-                )
-            return products
 
         def open_sum(k):
             bank = psum.tile([P, LUTS], F32, name="bank")
@@ -122,21 +105,39 @@ def tile_lutlayer_kernel(tc, x, w, w_comp, offs, out):
         def add_term(bank, term, last):
             nc.tensor.matmul(bank[:], identity[:], term, start=False, stop=last)
 
+        def multiply(b, i, count, buffers):
+            products = work.tile([P, count, LUTS], F32, name=f"products{i}", bufs=buffers)
+            for k in reversed(range(count)):
+                nc.vector.tensor_tensor(
+                    products[:, k, :],
+                    x_blocks[b][:].indirect(offsets[:, i * LIST_COLS : (i + 1) * LIST_COLS]),
+                    factors[b][:, k, :],
+                    MULT,
+                )
+            return products
+
+        upper_coef = held.tile([P, UPPER, LUTS], F32, name="upper_coef")
+        for k in reversed(range(UPPER)):
+            bank = psum.tile([P, LUTS], F32, name="bank")
+            nc.tensor.matmul(bank[:], to_coef_all[:, UPPER + k, :], sig_parts[:], start=True, stop=True)
+            nc.scalar.copy(upper_coef[:, k, :], bank[:])
+
+        factors = {b: upper_coef[:] for b in range(BLOCKS)}
+        sums = {}
+        all_but_last = {}
+
         def level_0(b):
-            factors[b] = coef[:, ENTRIES // 2 : ENTRIES, :]
-            products = multiply(b, 0, ENTRIES // 2)
-            finished = work.tile([P, LATE, LUTS], F32, name="finished0")
-            for k in reversed(range(LATE, 2 * LATE)):
-                bank = open_sum(k)
-                add_term(bank, products[:, k, :], last=True)
-                nc.scalar.copy(finished[:, k - LATE, :], bank[:])
-            for k in reversed(range(LATE)):
+            products = multiply(b, 0, 8, buffers=1)
+            finished = work.tile([P, 4, LUTS], F32, name="finished0")
+            for k in reversed(range(8)):
                 sums[b, k] = open_sum(k)
-                add_term(sums[b, k], products[:, k, :], last=False)
+                add_term(sums[b, k], products[:, k, :], last=k >= 4)
+                if k >= 4:
+                    nc.scalar.copy(finished[:, k - 4, :], sums[b, k][:])
             factors[b] = finished[:]
 
         def level_1(b):
-            products = multiply(b, 1, 4)
+            products = multiply(b, 1, 4, buffers=2)
             finished = work.tile([P, 2, LUTS], F32, name="finished1")
             for k in reversed(range(4)):
                 add_term(sums[b, k], products[:, k, :], last=k >= 2)
@@ -145,7 +146,7 @@ def tile_lutlayer_kernel(tc, x, w, w_comp, offs, out):
             factors[b] = finished[:]
 
         def level_2(b):
-            products = multiply(b, 2, 2)
+            products = multiply(b, 2, 2, buffers=2)
             finished = work.tile([P, 2, LUTS], F32, name="finished2")
             for k in reversed(range(2)):
                 add_term(sums[b, k], products[:, k, :], last=True)
@@ -154,13 +155,17 @@ def tile_lutlayer_kernel(tc, x, w, w_comp, offs, out):
             all_but_last[b] = finished[:, 0, :]
 
         def level_3(b):
-            products = multiply(b, 3, 1)
+            products = multiply(b, 3, 1, buffers=2)
             nc.vector.tensor_tensor(products[:, 0, :], all_but_last[b], products[:, 0, :], ADD)
             nc.sync.dma_start(out[b * P : (b + 1) * P, :], products[:, 0, :])
 
-        take_level = {0: level_0, 1: level_1, 2: level_2, 3: level_3}
+        blocks = range(BLOCKS)
         for step in range(BLOCKS + FAN_IN - 1):
-            for i in (2, 3, 1, 0):
-                b = step - i
-                if 0 <= b < BLOCKS:
-                    take_level[i](b)
+            if step - 2 in blocks:
+                level_2(step - 2)
+            if step - 3 in blocks:
+                level_3(step - 3)
+            if step - 1 in blocks:
+                level_1(step - 1)
+            if step in blocks:
+                level_0(step)

@@ -22,6 +22,7 @@ LUTS = 512
 LIST_COLS = LUTS // 16
 PARTS = 3
 ROWS = PARTS * ENTRIES
+GROUPS = LUTS // P
 BANKS = 8
 
 
@@ -71,8 +72,8 @@ def tile_lutlayer_kernel(tc, x, w, w_comp, offs, out):
             pattern=[[-ENTRIES, PARTS - 1]],
             channel_multiplier=1,
         )
-        sig_parts = held.tile([P, LUTS], BF16, name="sig_parts")
-        nc.gpsimd.memset(sig_parts[:], 0.0)
+        parts = held.tile([P, LUTS], F32, name="parts")
+        nc.gpsimd.memset(parts[:], 0.0)
         identity = held.tile([P, P], F32, name="identity")
         make_identity(nc, identity[:])
 
@@ -81,91 +82,147 @@ def tile_lutlayer_kernel(tc, x, w, w_comp, offs, out):
             to_coef_all[:, UPPER:ENTRIES, :], to_coef[:, UPPER:ENTRIES].unsqueeze(2).to_broadcast([P, UPPER, P])
         )
 
+        def upper_half(tile):
+            return tile.bitcast(BF16).rearrange("p (n two) -> p n two", two=2)[:, :, 1]
+
         logit = held.tile([ROWS, LUTS], F32, name="logit")
         nc.vector.tensor_tensor(logit[:], w_rows[:], w_comp_rows[:], SUBTRACT)
         sig = held.tile([ROWS, LUTS], F32, name="sig")
         nc.scalar.activation(sig[:], logit[:], SIGMOID)
         nc.scalar.copy(to_coef_all[:, 0:UPPER, :], to_coef[:, 0:UPPER].unsqueeze(2).to_broadcast([P, UPPER, P]))
-        head = held.tile([ROWS, LUTS], BF16, name="head")
-        nc.vector.tensor_copy(head[:], sig[:])
         after_head = held.tile([ROWS, LUTS], F32, name="after_head")
-        nc.vector.scalar_tensor_tensor(after_head[:], head[:], minus_from[0:ROWS, 0:1], sig[:], MULT, ADD)
-        middle = held.tile([ROWS, LUTS], BF16, name="middle")
-        nc.vector.tensor_copy(middle[:], after_head[:])
         nc.vector.scalar_tensor_tensor(
-            sig_parts[0:ROWS, :], middle[:], minus_from[0:ROWS, 1:2], after_head[:], MULT, ADD
+            after_head[:], upper_half(sig[:]), minus_from[0:ROWS, 0:1], sig[:], MULT, ADD
         )
+        nc.vector.scalar_tensor_tensor(
+            parts[0:ROWS, :], upper_half(after_head[:]), minus_from[0:ROWS, 1:2], after_head[:], MULT, ADD
+        )
+        sig_parts = upper_half(parts[:])
 
 
         def open_sum(k):
             bank = psum.tile([P, LUTS], F32, name="bank")
-            nc.tensor.matmul(bank[:], to_coef_all[:, k, :], sig_parts[:], start=True, stop=False)
+            nc.tensor.matmul(bank[:], to_coef_all[:, k, :], sig_parts, start=True, stop=False)
             return bank
 
         def add_term(bank, term, last):
             nc.tensor.matmul(bank[:], identity[:], term, start=False, stop=last)
 
-        def multiply(b, i, count, buffers):
-            products = work.tile([P, count, LUTS], F32, name=f"products{i}", bufs=buffers)
-            for k in reversed(range(count)):
+        def multiply(b, i, ks):
+            by_k = {}
+            if max(ks):
+                products = work.tile([P, max(ks), LUTS], F32, name=f"products{i}", bufs=2 if i else 1)
+            for k in ks:
+                if k:
+                    by_k[k] = products[:, k - 1, :]
+                else:
+                    term = work.tile([P, LUTS], F32, name=f"term{i}", bufs=1 if i == 0 else FAN_IN - i)
+                    by_k[k] = terms[b, i] = term[:]
                 nc.vector.tensor_tensor(
-                    products[:, k, :],
+                    by_k[k],
                     x_blocks[b][:].indirect(offsets[:, i * LIST_COLS : (i + 1) * LIST_COLS]),
-                    factors[b][:, k, :],
+                    factors[b, i][:, k, :],
                     MULT,
                 )
-            return products
+            return by_k
+
+        def flip_terms(b):
+            bank = psum.tile([P, GROUPS, P], F32, name="bank")
+            for g in range(GROUPS):
+                for i in range(FAN_IN):
+                    nc.tensor.matmul(
+                        bank[:, g, :],
+                        terms[b, i][:, g * P : (g + 1) * P],
+                        identity[:],
+                        start=i == 0,
+                        stop=i == FAN_IN - 1,
+                        is_transpose=True,
+                    )
+            flipped = work.tile([P, GROUPS, P], F32, name="flipped")
+            nc.scalar.copy(flipped[:], bank[:])
+            return flipped
+
+        def flip_back(flipped):
+            bank = open_sum(0)
+            for g in range(GROUPS):
+                nc.tensor.matmul(
+                    bank[:, g * P : (g + 1) * P],
+                    flipped[:, g, :],
+                    identity[:],
+                    start=False,
+                    stop=g == GROUPS - 1,
+                    is_transpose=True,
+                )
+            return bank
 
         upper_coef = held.tile([P, UPPER, LUTS], F32, name="upper_coef")
         for k in reversed(range(UPPER)):
             bank = psum.tile([P, LUTS], F32, name="bank")
-            nc.tensor.matmul(bank[:], to_coef_all[:, UPPER + k, :], sig_parts[:], start=True, stop=True)
+            nc.tensor.matmul(bank[:], to_coef_all[:, UPPER + k, :], sig_parts, start=True, stop=True)
             nc.scalar.copy(upper_coef[:, k, :], bank[:])
 
-        factors = {b: upper_coef[:] for b in range(BLOCKS)}
+        factors = {(b, 0): upper_coef[:] for b in range(BLOCKS)}
         sums = {}
-        all_but_last = {}
+        terms = {}
+        flipped_sums = {}
+        LAST = BLOCKS - 1
 
         def level_0(b):
-            products = multiply(b, 0, 8, buffers=1)
+            products = multiply(b, 0, range(7, 0, -1))
             finished = work.tile([P, 4, LUTS], F32, name="finished0")
-            for k in reversed(range(8)):
+            for k in range(7, 0, -1):
                 sums[b, k] = open_sum(k)
-                add_term(sums[b, k], products[:, k, :], last=k >= 4)
+                add_term(sums[b, k], products[k], last=k >= 4)
                 if k >= 4:
                     nc.scalar.copy(finished[:, k - 4, :], sums[b, k][:])
-            factors[b] = finished[:]
+            factors[b, 1] = finished[:]
 
         def level_1(b):
-            products = multiply(b, 1, 4, buffers=2)
+            products = multiply(b, 1, range(3, -1, -1))
             finished = work.tile([P, 2, LUTS], F32, name="finished1")
-            for k in reversed(range(4)):
-                add_term(sums[b, k], products[:, k, :], last=k >= 2)
+            for k in range(3, 0, -1):
+                add_term(sums[b, k], products[k], last=k >= 2)
                 if k >= 2:
                     nc.scalar.copy(finished[:, k - 2, :], sums[b, k][:])
-            factors[b] = finished[:]
+            factors[b, 2] = finished[:]
+            if b == LAST:
+                sums[b, 0] = open_sum(0)
+                add_term(sums[b, 0], products[0], last=False)
 
         def level_2(b):
-            products = multiply(b, 2, 2, buffers=2)
-            finished = work.tile([P, 2, LUTS], F32, name="finished2")
-            for k in reversed(range(2)):
-                add_term(sums[b, k], products[:, k, :], last=True)
-                nc.scalar.copy(finished[:, k, :], sums[b, k][:])
-            factors[b] = finished[:, 1:2, :]
-            all_but_last[b] = finished[:, 0, :]
+            products = multiply(b, 2, range(1, -1, -1))
+            finished = work.tile([P, 1, LUTS], F32, name="finished2")
+            add_term(sums[b, 1], products[1], last=True)
+            nc.scalar.copy(finished[:, 0, :], sums[b, 1][:])
+            factors[b, 3] = finished[:]
+            if b == LAST:
+                add_term(sums[b, 0], products[0], last=False)
 
         def level_3(b):
-            products = multiply(b, 3, 1, buffers=2)
-            nc.vector.tensor_tensor(products[:, 0, :], all_but_last[b], products[:, 0, :], ADD)
-            nc.sync.dma_start(out[b * P : (b + 1) * P, :], products[:, 0, :])
+            multiply(b, 0, [0])
+            if b == LAST:
+                add_term(sums[b, 0], terms[b, 0], last=True)
+            multiply(b, 3, [0])
+            if b != LAST:
+                flipped_sums[b] = flip_terms(b)
+
+        def store(b):
+            result = work.tile([P, LUTS], F32, name="result")
+            if b != LAST:
+                nc.scalar.copy(result[:], flip_back(flipped_sums[b])[:])
+            else:
+                nc.vector.tensor_tensor(result[:], sums[b, 0][:], terms[b, 3], ADD)
+            nc.sync.dma_start(out[b * P : (b + 1) * P, :], result[:])
 
         blocks = range(BLOCKS)
         for step in range(BLOCKS + FAN_IN - 1):
-            if step - 2 in blocks:
-                level_2(step - 2)
             if step - 3 in blocks:
                 level_3(step - 3)
+            if step - 2 in blocks:
+                level_2(step - 2)
             if step - 1 in blocks:
                 level_1(step - 1)
+            if step - 3 in blocks:
+                store(step - 3)
             if step in blocks:
                 level_0(step)

@@ -19,6 +19,7 @@ FAN_IN = 4
 ENTRIES = 16
 UPPER = ENTRIES // 2
 LUTS = 512
+HALVES = [slice(0, LUTS // 2), slice(LUTS // 2, LUTS)]
 LIST_COLS = LUTS // 16
 PARTS = 3
 ROWS = PARTS * ENTRIES
@@ -46,7 +47,7 @@ def tile_lutlayer_kernel(tc, x, w, w_comp, offs, out):
             nc.sync.dma_start(x_block[:], x[b * P : (b + 1) * P, :])
             x_blocks.append(x_block)
 
-        to_coef = held.tile([P, ENTRIES], F32, name="to_coef")
+        to_coef = held.tile([P, ENTRIES], BF16, name="to_coef")
         nc.gpsimd.memset(to_coef[:], 0.0)
         for part in range(PARTS):
             nc.gpsimd.affine_select(
@@ -77,32 +78,38 @@ def tile_lutlayer_kernel(tc, x, w, w_comp, offs, out):
         identity = held.tile([P, P], F32, name="identity")
         make_identity(nc, identity[:])
 
-        to_coef_all = held.tile([P, ENTRIES, P], BF16, name="to_coef_all")
-        nc.scalar.copy(
-            to_coef_all[:, UPPER:ENTRIES, :], to_coef[:, UPPER:ENTRIES].unsqueeze(2).to_broadcast([P, UPPER, P])
-        )
+        def spread(k):
+            return to_coef[:, k : k + 1].to_broadcast([P, P])
 
         def upper_half(tile):
             return tile.bitcast(BF16).rearrange("p (n two) -> p n two", two=2)[:, :, 1]
 
         logit = held.tile([ROWS, LUTS], F32, name="logit")
-        nc.vector.tensor_tensor(logit[:], w_rows[:], w_comp_rows[:], SUBTRACT)
         sig = held.tile([ROWS, LUTS], F32, name="sig")
-        nc.scalar.activation(sig[:], logit[:], SIGMOID)
-        nc.scalar.copy(to_coef_all[:, 0:UPPER, :], to_coef[:, 0:UPPER].unsqueeze(2).to_broadcast([P, UPPER, P]))
         after_head = held.tile([ROWS, LUTS], F32, name="after_head")
-        nc.vector.scalar_tensor_tensor(
-            after_head[:], upper_half(sig[:]), minus_from[0:ROWS, 0:1], sig[:], MULT, ADD
-        )
-        nc.vector.scalar_tensor_tensor(
-            parts[0:ROWS, :], upper_half(after_head[:]), minus_from[0:ROWS, 1:2], after_head[:], MULT, ADD
-        )
+        for cols in HALVES:
+            nc.vector.tensor_tensor(logit[:, cols], w_rows[:, cols], w_comp_rows[:, cols], SUBTRACT)
+        for cols in HALVES:
+            nc.scalar.activation(sig[:, cols], logit[:, cols], SIGMOID)
+        for cols in HALVES:
+            nc.vector.scalar_tensor_tensor(
+                after_head[:, cols], upper_half(sig[:, cols]), minus_from[0:ROWS, 0:1], sig[:, cols], MULT, ADD
+            )
+        for cols in HALVES:
+            nc.vector.scalar_tensor_tensor(
+                parts[0:ROWS, cols],
+                upper_half(after_head[:, cols]),
+                minus_from[0:ROWS, 1:2],
+                after_head[:, cols],
+                MULT,
+                ADD,
+            )
         sig_parts = upper_half(parts[:])
 
 
         def open_sum(k):
             bank = psum.tile([P, LUTS], F32, name="bank")
-            nc.tensor.matmul(bank[:], to_coef_all[:, k, :], sig_parts, start=True, stop=False)
+            nc.tensor.matmul(bank[:], spread(k), sig_parts, start=True, stop=False)
             return bank
 
         def add_term(bank, term, last):
@@ -156,9 +163,13 @@ def tile_lutlayer_kernel(tc, x, w, w_comp, offs, out):
             return bank
 
         upper_coef = held.tile([P, UPPER, LUTS], F32, name="upper_coef")
-        for k in reversed(range(UPPER)):
+        for cols, copy in zip(HALVES, (nc.scalar.copy, nc.vector.tensor_copy)):
             bank = psum.tile([P, LUTS], F32, name="bank")
-            nc.tensor.matmul(bank[:], to_coef_all[:, UPPER + k, :], sig_parts, start=True, stop=True)
+            nc.tensor.matmul(bank[:, cols], spread(ENTRIES - 1), sig_parts[:, cols], start=True, stop=True)
+            copy(upper_coef[:, UPPER - 1, cols], bank[:, cols])
+        for k in reversed(range(UPPER - 1)):
+            bank = psum.tile([P, LUTS], F32, name="bank")
+            nc.tensor.matmul(bank[:], spread(UPPER + k), sig_parts, start=True, stop=True)
             nc.scalar.copy(upper_coef[:, k, :], bank[:])
 
         factors = {(b, 0): upper_coef[:] for b in range(BLOCKS)}

@@ -37,7 +37,7 @@ def tile_lutlayer_kernel(tc, x, w, w_comp, offs, out):
         w_rows = held.tile([ROWS, LUTS], F32, name="w_rows")
         w_comp_rows = held.tile([ROWS, LUTS], F32, name="w_comp_rows")
         for part in range(PARTS):
-            nc.scalar.dma_start(w_rows[part * ENTRIES : (part + 1) * ENTRIES, :], w)
+            nc.sync.dma_start(w_rows[part * ENTRIES : (part + 1) * ENTRIES, :], w)
             nc.sync.dma_start(w_comp_rows[part * ENTRIES : (part + 1) * ENTRIES, :], w_comp)
         offsets = held.tile([P, FAN_IN * LIST_COLS], U16, name="offsets")
         nc.sync.dma_start(offsets[:], offs)
@@ -163,7 +163,7 @@ def tile_lutlayer_kernel(tc, x, w, w_comp, offs, out):
             return bank
 
         upper_coef = held.tile([P, UPPER, LUTS], F32, name="upper_coef")
-        for cols, copy in zip(HALVES, (nc.scalar.copy, nc.vector.tensor_copy)):
+        for cols, copy in zip(HALVES, (nc.vector.tensor_copy, nc.scalar.copy)):
             bank = psum.tile([P, LUTS], F32, name="bank")
             nc.tensor.matmul(bank[:, cols], spread(ENTRIES - 1), sig_parts[:, cols], start=True, stop=True)
             copy(upper_coef[:, UPPER - 1, cols], bank[:, cols])

@@ -20,7 +20,7 @@ ENTRIES = 16
 UPPER = ENTRIES // 2
 LUTS = 512
 HALVES = [slice(0, LUTS // 2), slice(LUTS // 2, LUTS)]
-LIST_COLS = LUTS // 16
+LIST_COLS = FAN_IN * LUTS // 16
 PARTS = 3
 ROWS = PARTS * ENTRIES
 GROUPS = LUTS // P
@@ -39,7 +39,7 @@ def tile_lutlayer_kernel(tc, x, w, w_comp, offs, out):
         for part in range(PARTS):
             nc.sync.dma_start(w_rows[part * ENTRIES : (part + 1) * ENTRIES, :], w)
             nc.sync.dma_start(w_comp_rows[part * ENTRIES : (part + 1) * ENTRIES, :], w_comp)
-        offsets = held.tile([P, FAN_IN * LIST_COLS], U16, name="offsets")
+        offsets = held.tile([P, LIST_COLS], U16, name="offsets")
         nc.sync.dma_start(offsets[:], offs)
         x_blocks = []
         for b in range(BLOCKS):
@@ -107,13 +107,19 @@ def tile_lutlayer_kernel(tc, x, w, w_comp, offs, out):
         sig_parts = upper_half(parts[:])
 
 
-        def open_sum(k):
+        ALL = slice(0, LUTS)
+
+        def open_sum(k, cols=ALL):
             bank = psum.tile([P, LUTS], F32, name="bank")
-            nc.tensor.matmul(bank[:], spread(k), sig_parts, start=True, stop=False)
+            nc.tensor.matmul(bank[:, cols], spread(k), sig_parts[:, cols], start=True, stop=False)
             return bank
 
-        def add_term(bank, term, last):
-            nc.tensor.matmul(bank[:], identity[:], term, start=False, stop=last)
+        def add_term(bank, term, last, cols=ALL):
+            nc.tensor.matmul(bank[:, cols], identity[:], term[:, cols], start=False, stop=last)
+
+        def add_to_last_value_0(term, last):
+            for cols, bank in zip(HALVES, last_value_0):
+                add_term(bank, term, last, cols)
 
         def multiply(b, i, ks):
             by_k = {}
@@ -125,12 +131,14 @@ def tile_lutlayer_kernel(tc, x, w, w_comp, offs, out):
                 else:
                     term = work.tile([P, LUTS], F32, name=f"term{i}", bufs=1 if i == 0 else FAN_IN - i)
                     by_k[k] = terms[b, i] = term[:]
-                nc.vector.tensor_tensor(
-                    by_k[k],
-                    x_blocks[b][:].indirect(offsets[:, i * LIST_COLS : (i + 1) * LIST_COLS]),
-                    factors[b, i][:, k, :],
-                    MULT,
-                )
+                for cols in HALVES if (b, i, k) == (0, 0, UPPER - 1) else [ALL]:
+                    first, last = ((i * LUTS + end) // 16 for end in (cols.start, cols.stop))
+                    nc.vector.tensor_tensor(
+                        by_k[k][:, cols],
+                        x_blocks[b][:].indirect(offsets[:, first:last]),
+                        factors[b, i][:, k, cols],
+                        MULT,
+                    )
             return by_k
 
         def flip_terms(b):
@@ -177,6 +185,7 @@ def tile_lutlayer_kernel(tc, x, w, w_comp, offs, out):
         terms = {}
         flipped_sums = {}
         LAST = BLOCKS - 1
+        last_value_0 = []
 
         def level_0(b):
             products = multiply(b, 0, range(7, 0, -1))
@@ -197,8 +206,8 @@ def tile_lutlayer_kernel(tc, x, w, w_comp, offs, out):
                     nc.scalar.copy(finished[:, k - 2, :], sums[b, k][:])
             factors[b, 2] = finished[:]
             if b == LAST:
-                sums[b, 0] = open_sum(0)
-                add_term(sums[b, 0], products[0], last=False)
+                last_value_0.extend(open_sum(0, cols) for cols in HALVES)
+                add_to_last_value_0(products[0], last=False)
 
         def level_2(b):
             products = multiply(b, 2, range(1, -1, -1))
@@ -207,12 +216,12 @@ def tile_lutlayer_kernel(tc, x, w, w_comp, offs, out):
             nc.scalar.copy(finished[:, 0, :], sums[b, 1][:])
             factors[b, 3] = finished[:]
             if b == LAST:
-                add_term(sums[b, 0], products[0], last=False)
+                add_to_last_value_0(products[0], last=False)
 
         def level_3(b):
             multiply(b, 0, [0])
             if b == LAST:
-                add_term(sums[b, 0], terms[b, 0], last=True)
+                add_to_last_value_0(terms[b, 0], last=True)
             multiply(b, 3, [0])
             if b != LAST:
                 flipped_sums[b] = flip_terms(b)
@@ -222,7 +231,8 @@ def tile_lutlayer_kernel(tc, x, w, w_comp, offs, out):
             if b != LAST:
                 nc.scalar.copy(result[:], flip_back(flipped_sums[b])[:])
             else:
-                nc.vector.tensor_tensor(result[:], sums[b, 0][:], terms[b, 3], ADD)
+                for cols, bank in zip(HALVES, last_value_0):
+                    nc.vector.tensor_tensor(result[:, cols], bank[:, cols], terms[b, 3][:, cols], ADD)
             nc.sync.dma_start(out[b * P : (b + 1) * P, :], result[:])
 
         blocks = range(BLOCKS)

@@ -143,14 +143,15 @@ def tile_lutlayer_kernel(tc, x, w, w_comp, offs, out):
 
         def flip_terms(b):
             bank = psum.tile([P, GROUPS, P], F32, name="bank")
-            for g in range(GROUPS):
-                for i in range(FAN_IN):
+            as_they_come = (1, 2, 0, 3)
+            for i in as_they_come:
+                for g in range(GROUPS):
                     nc.tensor.matmul(
                         bank[:, g, :],
                         terms[b, i][:, g * P : (g + 1) * P],
                         identity[:],
-                        start=i == 0,
-                        stop=i == FAN_IN - 1,
+                        start=(i, g) == (as_they_come[0], 0),
+                        stop=(i, g) == (as_they_come[-1], GROUPS - 1),
                         is_transpose=True,
                     )
             flipped = work.tile([P, GROUPS, P], F32, name="flipped")

@@ -95,7 +95,6 @@ def tile_lutlayer_kernel(tc, x, w, w_comp, offs, out):
             nc.vector.scalar_tensor_tensor(
                 after_head[:, cols], upper_half(sig[:, cols]), minus_from[0:ROWS, 0:1], sig[:, cols], MULT, ADD
             )
-        for cols in HALVES:
             nc.vector.scalar_tensor_tensor(
                 parts[0:ROWS, cols],
                 upper_half(after_head[:, cols]),
@@ -172,10 +171,10 @@ def tile_lutlayer_kernel(tc, x, w, w_comp, offs, out):
             return bank
 
         upper_coef = held.tile([P, UPPER, LUTS], F32, name="upper_coef")
-        for cols, copy in zip(HALVES, (nc.vector.tensor_copy, nc.scalar.copy)):
+        for cols in HALVES:
             bank = psum.tile([P, LUTS], F32, name="bank")
             nc.tensor.matmul(bank[:, cols], spread(ENTRIES - 1), sig_parts[:, cols], start=True, stop=True)
-            copy(upper_coef[:, UPPER - 1, cols], bank[:, cols])
+            nc.scalar.copy(upper_coef[:, UPPER - 1, cols], bank[:, cols])
         for k in reversed(range(UPPER - 1)):
             bank = psum.tile([P, LUTS], F32, name="bank")
             nc.tensor.matmul(bank[:], spread(UPPER + k), sig_parts, start=True, stop=True)

@@ -130,7 +130,7 @@ def tile_lutlayer_kernel(tc, x, w, w_comp, offs, out):
                 else:
                     term = work.tile([P, LUTS], F32, name=f"term{i}", bufs=1 if i == 0 else FAN_IN - i)
                     by_k[k] = terms[b, i] = term[:]
-                for cols in HALVES if (b, i, k) == (0, 0, UPPER - 1) else [ALL]:
+                for cols in HALVES if (b, i, k) in ((0, 0, UPPER - 1), (LAST, 3, 0)) else [ALL]:
                     first, last = ((i * LUTS + end) // 16 for end in (cols.start, cols.stop))
                     nc.vector.tensor_tensor(
                         by_k[k][:, cols],

import concourse.mybir as mybir
from concourse.masks import make_identity

F32 = mybir.dt.float32
BF16 = mybir.dt.bfloat16
U16 = mybir.dt.uint16
MULT = mybir.AluOpType.mult
ADD = mybir.AluOpType.add
SUBTRACT = mybir.AluOpType.subtract
NOT_EQUAL = mybir.AluOpType.not_equal
IS_GE = mybir.AluOpType.is_ge
SIGMOID = mybir.ActivationFunctionType.Sigmoid

P = 128
SAMPLES = 512
BLOCKS = SAMPLES // P
INPUTS = 512
FAN_IN = 4
ENTRIES = 16
UPPER = ENTRIES // 2
LUTS = 512
HALVES = [slice(0, LUTS // 2), slice(LUTS // 2, LUTS)]
LIST_COLS = FAN_IN * LUTS // 16
PARTS = 3
ROWS = PARTS * ENTRIES
GROUPS = LUTS // P
BANKS = 8


def tile_lutlayer_kernel(tc, x, w, w_comp, offs, out):
    nc = tc.nc
    with (
        tc.tile_pool(name="held", bufs=1) as held,
        tc.tile_pool(name="work", bufs=2) as work,
        tc.psum_pool(name="psum", bufs=BANKS) as psum,
    ):
        w_rows = held.tile([ROWS, LUTS], F32, name="w_rows")
        w_comp_rows = held.tile([ROWS, LUTS], F32, name="w_comp_rows")
        for part in range(PARTS):
            nc.sync.dma_start(w_rows[part * ENTRIES : (part + 1) * ENTRIES, :], w)
            nc.sync.dma_start(w_comp_rows[part * ENTRIES : (part + 1) * ENTRIES, :], w_comp)
        offsets = held.tile([P, LIST_COLS], U16, name="offsets")
        nc.sync.dma_start(offsets[:], offs)
        x_blocks = []
        for b in range(BLOCKS):
            x_block = held.tile([P, INPUTS], F32, name=f"x_block{b}")
            nc.sync.dma_start(x_block[:], x[b * P : (b + 1) * P, :])
            x_blocks.append(x_block)

        to_coef = held.tile([P, ENTRIES], BF16, name="to_coef")
        nc.gpsimd.memset(to_coef[:], 0.0)
        for part in range(PARTS):
            nc.gpsimd.affine_select(
                out=to_coef[:],
                in_=to_coef[:],
                compare_op=NOT_EQUAL,
                fill=1.0,
                base=-part * ENTRIES,
                pattern=[[-1, ENTRIES]],
                channel_multiplier=1,
            )
        for bit in range(FAN_IN):
            pairs = to_coef[:].rearrange("t (g two h) -> t g two h", two=2, h=1 << bit)
            nc.gpsimd.tensor_tensor(pairs[:, :, 1:2, :], pairs[:, :, 1:2, :], pairs[:, :, 0:1, :], SUBTRACT)
        minus_from = held.tile([P, PARTS - 1], F32, name="minus_from")
        nc.gpsimd.memset(minus_from[:], -1.0)
        nc.gpsimd.affine_select(
            out=minus_from[:],
            in_=minus_from[:],
            compare_op=IS_GE,
            fill=0.0,
            base=-ENTRIES,
            pattern=[[-ENTRIES, PARTS - 1]],
            channel_multiplier=1,
        )
        parts = held.tile([P, LUTS], F32, name="parts")
        nc.gpsimd.memset(parts[:], 0.0)
        identity = held.tile([P, P], F32, name="identity")
        make_identity(nc, identity[:])

        def spread(k):
            return to_coef[:, k : k + 1].to_broadcast([P, P])

        def upper_half(tile):
            return tile.bitcast(BF16).rearrange("p (n two) -> p n two", two=2)[:, :, 1]

        logit = held.tile([ROWS, LUTS], F32, name="logit")
        sig = held.tile([ROWS, LUTS], F32, name="sig")
        after_head = held.tile([ROWS, LUTS], F32, name="after_head")
        for cols in HALVES:
            nc.vector.tensor_tensor(logit[:, cols], w_rows[:, cols], w_comp_rows[:, cols], SUBTRACT)
        for cols in HALVES:
            nc.scalar.activation(sig[:, cols], logit[:, cols], SIGMOID)
        for cols in HALVES:
            nc.vector.scalar_tensor_tensor(
                after_head[:, cols], upper_half(sig[:, cols]), minus_from[0:ROWS, 0:1], sig[:, cols], MULT, ADD
            )
            nc.vector.scalar_tensor_tensor(
                parts[0:ROWS, cols],
                upper_half(after_head[:, cols]),
                minus_from[0:ROWS, 1:2],
                after_head[:, cols],
                MULT,
                ADD,
            )
        sig_parts = upper_half(parts[:])


        ALL = slice(0, LUTS)

        def open_sum(k, cols=ALL):
            bank = psum.tile([P, LUTS], F32, name="bank")
            nc.tensor.matmul(bank[:, cols], spread(k), sig_parts[:, cols], start=True, stop=False)
            return bank

        def add_term(bank, term, last, cols=ALL):
            nc.tensor.matmul(bank[:, cols], identity[:], term[:, cols], start=False, stop=last)

        def add_to_last_value_0(term, last):
            for cols, bank in zip(HALVES, last_value_0):
                add_term(bank, term, last, cols)

        def multiply(b, i, ks):
            by_k = {}
            if max(ks):
                products = work.tile([P, max(ks), LUTS], F32, name=f"products{i}", bufs=2 if i else 1)
            for k in ks:
                if k:
                    by_k[k] = products[:, k - 1, :]
                else:
                    term = work.tile([P, LUTS], F32, name=f"term{i}", bufs=1 if i == 0 else FAN_IN - i)
                    by_k[k] = terms[b, i] = term[:]
                for cols in HALVES if (b, i, k) in ((0, 0, UPPER - 1), (LAST, 3, 0)) else [ALL]:
                    first, last = ((i * LUTS + end) // 16 for end in (cols.start, cols.stop))
                    nc.vector.tensor_tensor(
                        by_k[k][:, cols],
                        x_blocks[b][:].indirect(offsets[:, first:last]),
                        factors[b, i][:, k, cols],
                        MULT,
                    )
            return by_k

        def flip_terms(b):
            bank = psum.tile([P, GROUPS, P], F32, name="bank")
            as_they_come = (1, 2, 0, 3)
            for i in as_they_come:
                for g in range(GROUPS):
                    nc.tensor.matmul(
                        bank[:, g, :],
                        terms[b, i][:, g * P : (g + 1) * P],
                        identity[:],
                        start=(i, g) == (as_they_come[0], 0),
                        stop=(i, g) == (as_they_come[-1], GROUPS - 1),
                        is_transpose=True,
                    )
            flipped = work.tile([P, GROUPS, P], F32, name="flipped")
            nc.scalar.copy(flipped[:], bank[:])
            return flipped

        def flip_back(flipped):
            bank = open_sum(0)
            for g in range(GROUPS):
                nc.tensor.matmul(
                    bank[:, g * P : (g + 1) * P],
                    flipped[:, g, :],
                    identity[:],
                    start=False,
                    stop=g == GROUPS - 1,
                    is_transpose=True,
                )
            return bank

        upper_coef = held.tile([P, UPPER, LUTS], F32, name="upper_coef")
        for cols in HALVES:
            bank = psum.tile([P, LUTS], F32, name="bank")
            nc.tensor.matmul(bank[:, cols], spread(ENTRIES - 1), sig_parts[:, cols], start=True, stop=True)
            nc.scalar.copy(upper_coef[:, UPPER - 1, cols], bank[:, cols])
        for k in reversed(range(UPPER - 1)):
            bank = psum.tile([P, LUTS], F32, name="bank")
            nc.tensor.matmul(bank[:], spread(UPPER + k), sig_parts, start=True, stop=True)
            nc.scalar.copy(upper_coef[:, k, :], bank[:])

        factors = {(b, 0): upper_coef[:] for b in range(BLOCKS)}
        sums = {}
        terms = {}
        flipped_sums = {}
        LAST = BLOCKS - 1
        last_value_0 = []

        def level_0(b):
            products = multiply(b, 0, range(7, 0, -1))
            finished = work.tile([P, 4, LUTS], F32, name="finished0")
            for k in range(7, 0, -1):
                sums[b, k] = open_sum(k)
                add_term(sums[b, k], products[k], last=k >= 4)
                if k >= 4:
                    nc.scalar.copy(finished[:, k - 4, :], sums[b, k][:])
            factors[b, 1] = finished[:]

        def level_1(b):
            products = multiply(b, 1, range(3, -1, -1))
            finished = work.tile([P, 2, LUTS], F32, name="finished1")
            for k in range(3, 0, -1):
                add_term(sums[b, k], products[k], last=k >= 2)
                if k >= 2:
                    nc.scalar.copy(finished[:, k - 2, :], sums[b, k][:])
            factors[b, 2] = finished[:]
            if b == LAST:
                last_value_0.extend(open_sum(0, cols) for cols in HALVES)
                add_to_last_value_0(products[0], last=False)

        def level_2(b):
            products = multiply(b, 2, range(1, -1, -1))
            finished = work.tile([P, 1, LUTS], F32, name="finished2")
            add_term(sums[b, 1], products[1], last=True)
            nc.scalar.copy(finished[:, 0, :], sums[b, 1][:])
            factors[b, 3] = finished[:]
            if b == LAST:
                add_to_last_value_0(products[0], last=False)

        def level_3(b):
            multiply(b, 0, [0])
            if b == LAST:
                add_to_last_value_0(terms[b, 0], last=True)
            multiply(b, 3, [0])
            if b != LAST:
                flipped_sums[b] = flip_terms(b)

        def store(b):
            result = work.tile([P, LUTS], F32, name="result")
            if b != LAST:
                nc.scalar.copy(result[:], flip_back(flipped_sums[b])[:])
            else:
                for cols, bank in zip(HALVES, last_value_0):
                    nc.vector.tensor_tensor(result[:, cols], bank[:, cols], terms[b, 3][:, cols], ADD)
            nc.sync.dma_start(out[b * P : (b + 1) * P, :], result[:])

        blocks = range(BLOCKS)
        for step in range(BLOCKS + FAN_IN - 1):
            if step - 3 in blocks:
                level_3(step - 3)
            if step - 2 in blocks:
                level_2(step - 2)
            if step - 1 in blocks:
                level_1(step - 1)
            if step - 3 in blocks:
                store(step - 3)
            if step in blocks:
                level_0(step)
